import numpy as np
import ml_dtypes


def mxq(x, axis, fmt="e4m3"):
    dtype, down = {"e4m3": (ml_dtypes.float8_e4m3fn, 7), "e5m2": (ml_dtypes.float8_e5m2, 14)}[fmt]
    v = np.moveaxis(np.asarray(x, np.float32).astype(ml_dtypes.bfloat16).astype(np.float64), axis, -1)
    blocks = v.reshape(v.shape[:-1] + (-1, 32))
    amax = np.abs(blocks).max(-1, keepdims=True)
    byte = np.maximum(np.where(amax > 0, np.frexp(amax)[1] - 1 + 127, 0) - down, 1)
    scale = np.exp2(byte - 127.0)
    codes = (blocks / scale).astype(np.float32).astype(dtype).astype(np.float64)
    return np.moveaxis((codes * scale).reshape(v.shape), -1, axis)


WIDE = False


def mx_kscale(k):
    if not WIDE:
        return np.ones(k)
    levels = np.array([10, -10, 5, -5, 0])
    a = np.random.permutation(np.resize(levels, k // 512 * 4)).reshape(k // 512, 4)
    idx = np.arange(k)
    return np.exp2(a[idx // 512, idx % 128 // 32])


BF16 = ml_dtypes.bfloat16


def bf(x):
    return np.asarray(x, np.float32).astype(BF16)


def f64(x):
    return np.asarray(x).astype(np.float64)


E2M1 = np.array([0.0, 0.5, 1.0, 1.5, 2.0, 3.0, 4.0, 6.0, -0.0, -0.5, -1.0, -1.5, -2.0, -3.0, -4.0, -6.0])


def pack_weight(w, fmt):
    k, n = w.shape
    w = f64(bf(w)).reshape(k // 32, 32, n)
    amax = np.abs(w).max(1)
    if fmt == "e4m3":
        byte = np.frexp(amax)[1] - 1 + 127 - 7
    else:
        mant, ex = np.frexp(amax / 6.0)
        byte = np.where(mant > 0.5, ex, ex - 1) + 127
    byte = np.clip(np.where(amax > 0, byte, 1), 1, 254)
    scaled = (w * np.exp2(127.0 - byte)[:, None, :]).reshape(k, n).astype(np.float32)
    by_word = np.ascontiguousarray(scaled.reshape(k // 512, 128, 4, n).transpose(0, 1, 3, 2))
    if fmt == "e4m3":
        words = by_word.astype(ml_dtypes.float8_e4m3fn).view(np.uint8)
    else:
        c = by_word.astype(ml_dtypes.float4_e2m1fn).view(np.uint8) & 0xF
        words = c[..., 0::2] | (c[..., 1::2] << 4)
    return np.ascontiguousarray(words), np.ascontiguousarray(byte.astype(np.uint8).reshape(k // 512, 16, n))


def unpack_weight(words, scales, fmt):
    g, p, n, _ = words.shape
    if fmt == "e4m3":
        vals = np.ascontiguousarray(words).view(ml_dtypes.float8_e4m3fn).astype(np.float64)
    else:
        nib = np.empty((g, p, n, 4), np.uint8)
        nib[..., 0::2] = words & 0xF
        nib[..., 1::2] = words >> 4
        vals = E2M1[nib]
    vals = vals * np.repeat(np.exp2(scales.astype(np.float64) - 127.0), 8, axis=1)[..., None]
    return vals.transpose(0, 1, 3, 2).reshape(g * 512, n)


B, C, H, W = 1, 4096, 8, 16
GAMMA_INIT = 0.1


def setup_inputs():
    t = np.exp2(np.round(np.log2(mx_kscale(C)) / 2))
    gain = np.exp(0.5 * np.random.standard_normal((B, 1, H, W)))
    x = np.random.standard_normal((B, C, H, W)) * gain * t[None, :, None, None]
    gamma = (GAMMA_INIT * np.eye(C) + np.abs(np.random.standard_normal((C, C))) / C) / (t * t)[None, :]
    beta = 0.5 + np.random.random(C)
    gamma_words, gamma_scales = pack_weight(np.ascontiguousarray(gamma.T), "e4m3")
    return {"x": bf(x), "gamma_words": gamma_words, "gamma_scales": gamma_scales, "beta": bf(beta)}


def reference(x, gamma_words, gamma_scales, beta):
    xf = f64(x)
    sq = (xf * xf).reshape(B, C, H * W)
    norm = (unpack_weight(gamma_words, gamma_scales, "e4m3").T @ mxq(sq, 1, "e4m3")) + f64(beta)[None, :, None]
    return xf / np.sqrt(norm.reshape(B, C, H, W))

@@ -1,0 +1,132 @@
+from contextlib import ExitStack
+
+import concourse.mybir as mybir
+from concourse.masks import make_identity
+
+FLOPS = 2 * 4096 * 4096 * 128
+
+F32 = mybir.dt.float32
+BF16 = mybir.dt.bfloat16
+I32 = mybir.dt.int32
+U32 = mybir.dt.uint32
+U8 = mybir.dt.uint8
+FP8X4 = mybir.dt.float8_e4m3fn_x4
+ACT = mybir.ActivationFunctionType
+ALU = mybir.AluOpType
+
+P = 128
+C = 4096
+G = 8
+NB = 512
+
+
+def tile_gdn_w_kernel(tc, x, gamma_words, gamma_scales, beta, out):
+    nc = tc.nc
+    xv = x.rearrange("b c h w -> (b c) (h w)").rearrange("(g p t) n -> p g (t n)", p=P, t=4)
+    ov = out.rearrange("b c h w -> (b c) (h w)").rearrange("(g p t) n -> p g (t n)", p=P, t=4)
+    with ExitStack() as ctx:
+        keep = ctx.enter_context(tc.tile_pool(name="keep", bufs=1))
+        work = ctx.enter_context(tc.tile_pool(name="work", bufs=3))
+        outp = ctx.enter_context(tc.tile_pool(name="outp", bufs=8))
+        psum = ctx.enter_context(tc.psum_pool(name="psum", bufs=1))
+
+        planes = keep.tile([P, 2 * C], U8, align_bytes=64)
+        nc.vector.memset(planes[:].bitcast(I32), 0)
+        ones = keep.tile([P, P], BF16)
+        nc.vector.memset(ones[:], 1.0)
+        seed = keep.tile([P, 1], F32)
+        nc.vector.memset(seed[:], 1.0)
+        warm = keep.tile([P, 1], F32)
+        nc.scalar.activation(out=warm[:], in_=seed[:], func=ACT.Abs_reciprocal_sqrt)
+        brow = keep.tile([P, C], BF16)
+        nc.gpsimd.memset(brow[:].bitcast(F32), 0.0)
+        nc.gpsimd.dma_start(out=brow[0:1, :], in_=beta.rearrange("(o c) -> o c", o=1))
+        ident = keep.tile([P, P], F32)
+        make_identity(nc, ident[:])
+
+        xk = keep.tile([P, G, NB], BF16)
+        nc.sync.dma_start(out=xk[:], in_=xv)
+        for a in range(2):
+            for q in range(4):
+                nc.sync.dma_start(
+                    out=planes[32 * q : 32 * q + 16, a * C : (a + 1) * C].bitcast(I32),
+                    in_=gamma_scales[4 * a : 4 * a + 4, 4 * q : 4 * q + 4, :].bitcast(I32),
+                )
+        words = {}
+
+        def load_words(g, m0, m1):
+            t = keep.tile([P, (m1 - m0) * NB], U32, name="w%d_%d" % (g, m0), align_bytes=64)
+            nc.sync.dma_start(
+                out=t[:].bitcast(I32),
+                in_=gamma_words[g, :, m0 * NB : m1 * NB, :].rearrange("p n t -> p (n t)").bitcast(I32),
+            )
+            for m in range(m0, m1):
+                words[(g, m)] = t[:, (m - m0) * NB : (m - m0 + 1) * NB]
+
+        for g in range(G):
+            load_words(g, 0, 4)
+        for g in range(G - 1):
+            load_words(g, 4, 8)
+        for m in range(4, 8):
+            load_words(G - 1, m, m + 1)
+
+        beta_bc = keep.tile([P, G, 4, P], F32)
+        for m in range(G):
+            bp = psum.tile([P, NB], F32, tag="bank%d" % m, name="bp%d" % m)
+            nc.tensor.matmul(out=bp[:], lhsT=ones[:], rhs=brow[:, m * NB : (m + 1) * NB], start=True, stop=True)
+            nc.scalar.copy(out=beta_bc[:, m], in_=bp[:].rearrange("n (v i) -> n i v", i=4))
+
+        xk4 = xk[:].rearrange("p g (t n) -> p g t n", t=4)
+        grouped = keep.tile([P, G, P, 4], BF16, align_bytes=64)
+        codes = keep.tile([P, G * P], U32, align_bytes=64)
+        sqplane = keep.tile([P, G * P], U8, align_bytes=64)
+        for h in range(2):
+            src = xk4[:, 4 * h : 4 * h + 4].rearrange("p g t n -> p g n t")
+            nc.vector.tensor_tensor(out=grouped[:, 4 * h : 4 * h + 4], in0=src, in1=src, op=ALU.mult)
+        for h in range(2):
+            nc.vector.quantize_mx(
+                out=codes[:, 512 * h : 512 * (h + 1)].bitcast(FP8X4),
+                scales=sqplane[:, 512 * h : 512 * (h + 1)],
+                in_=grouped[:, 4 * h : 4 * h + 4].rearrange("p g n t -> p (g n t)"),
+            )
+
+        acc = {}
+
+        def mx(g, m):
+            if g == 0:
+                acc[m] = psum.tile([P, NB], F32, tag="bank%d" % m, name="acc%d" % m)
+            a, b = divmod(g, 4)
+            nc.tensor.matmul_mx(
+                out=acc[m][:],
+                lhsT=codes[:, g * P : (g + 1) * P].bitcast(FP8X4),
+                lhsT_scale=sqplane[:, g * P : (g + 1) * P],
+                rhs=words[(g, m)].bitcast(FP8X4),
+                rhs_scale=planes[4 * b : P, a * C + m * NB : a * C + (m + 1) * NB],
+                start=(g == 0),
+                stop=(g == G - 1),
+            )
+
+        def epilogue(m):
+            t = work.tile([P, 4, P], F32, name="t%d" % m, tag="t")
+            nc.vector.tensor_tensor(
+                out=t[:], in0=acc[m][:].rearrange("n (v i) -> n i v", i=4), in1=beta_bc[:, m], op=ALU.add
+            )
+            r = work.tile([P, 4, P], F32, name="r%d" % m, tag="r")
+            nc.scalar.activation(out=r[:], in_=t[:], func=ACT.Abs_reciprocal_sqrt)
+            tr = psum.tile([P, 4, P], F32, tag="bank%d" % m, name="tr%d" % m)
+            for i in range(4):
+                nc.tensor.transpose(tr[:, i, :], r[:, i, :], ident[:])
+            o = outp.tile([P, 4, P], F32, name="o%d" % m, tag="o")
+            nc.vector.tensor_tensor(out=o[:], in0=tr[:], in1=xk4[:, m], op=ALU.mult)
+            nc.sync.dma_start(out=ov[:, m, :], in_=o[:].rearrange("p t n -> p (t n)"))
+
+        for g in range(G):
+            for m in range(4):
+                mx(g, m)
+        for g in range(G):
+            for m in range(4, 8):
+                mx(g, m)
+            if g < 4:
+                epilogue(g)
+        for m in range(4, 8):
+            epilogue(m)

@@ -39,19 +39,23 @@ def tile_gdn_w_kernel(tc, x, gamma_words, gamma_scales, beta, out):
         warm = keep.tile([P, 1], F32)
         nc.scalar.activation(out=warm[:], in_=seed[:], func=ACT.Abs_reciprocal_sqrt)
         brow = keep.tile([P, C], BF16)
-        nc.gpsimd.memset(brow[:].bitcast(F32), 0.0)
-        nc.gpsimd.dma_start(out=brow[0:1, :], in_=beta.rearrange("(o c) -> o c", o=1))
+        nc.vector.memset(brow[:].bitcast(I32), 0)
+        nc.scalar.dma_start(out=brow[0:1, :], in_=beta.rearrange("(o c) -> o c", o=1))
+
+        def load_planes(a):
+            for q in range(4):
+                nc.gpsimd.dma_start(
+                    out=planes[32 * q : 32 * q + 16, a * C : (a + 1) * C].bitcast(F32),
+                    in_=gamma_scales[4 * a : 4 * a + 4, 4 * q : 4 * q + 4, :].bitcast(F32),
+                )
+
+        load_planes(0)
+        load_planes(1)
         ident = keep.tile([P, P], F32)
         make_identity(nc, ident[:])
 
         xk = keep.tile([P, G, NB], BF16)
         nc.sync.dma_start(out=xk[:], in_=xv)
-        for a in range(2):
-            for q in range(4):
-                nc.sync.dma_start(
-                    out=planes[32 * q : 32 * q + 16, a * C : (a + 1) * C].bitcast(I32),
-                    in_=gamma_scales[4 * a : 4 * a + 4, 4 * q : 4 * q + 4, :].bitcast(I32),
-                )
         words = {}
 
         def load_words(g, m0, m1):

@@ -25,32 +25,29 @@ def tile_gdn_w_kernel(tc, x, gamma_words, gamma_scales, beta, out):
     xv = x.rearrange("b c h w -> (b c) (h w)").rearrange("(g p t) n -> p g (t n)", p=P, t=4)
     ov = out.rearrange("b c h w -> (b c) (h w)").rearrange("(g p t) n -> p g (t n)", p=P, t=4)
     with ExitStack() as ctx:
+        ctx.enter_context(tc.manual_schedule())
         keep = ctx.enter_context(tc.tile_pool(name="keep", bufs=1))
-        work = ctx.enter_context(tc.tile_pool(name="work", bufs=3))
+        work = ctx.enter_context(tc.tile_pool(name="work", bufs=6))
         outp = ctx.enter_context(tc.tile_pool(name="outp", bufs=8))
         psum = ctx.enter_context(tc.psum_pool(name="psum", bufs=1))
 
         planes = keep.tile([P, 2 * C], U8, align_bytes=64)
         nc.vector.memset(planes[:].bitcast(I32), 0)
+        brow = keep.tile([P, C], BF16)
+        nc.vector.memset(brow[:].bitcast(I32), 0)
         ones = keep.tile([P, P], BF16)
         nc.vector.memset(ones[:], 1.0)
         seed = keep.tile([P, 1], F32)
         nc.vector.memset(seed[:], 1.0)
         warm = keep.tile([P, 1], F32)
         nc.scalar.activation(out=warm[:], in_=seed[:], func=ACT.Abs_reciprocal_sqrt)
-        brow = keep.tile([P, C], BF16)
-        nc.vector.memset(brow[:].bitcast(I32), 0)
         nc.scalar.dma_start(out=brow[0:1, :], in_=beta.rearrange("(o c) -> o c", o=1))
-
-        def load_planes(a):
+        for a in range(2):
             for q in range(4):
                 nc.gpsimd.dma_start(
                     out=planes[32 * q : 32 * q + 16, a * C : (a + 1) * C].bitcast(F32),
                     in_=gamma_scales[4 * a : 4 * a + 4, 4 * q : 4 * q + 4, :].bitcast(F32),
                 )
-
-        load_planes(0)
-        load_planes(1)
         ident = keep.tile([P, P], F32)
         make_identity(nc, ident[:])
 
@@ -95,6 +92,8 @@ def tile_gdn_w_kernel(tc, x, gamma_words, gamma_scales, beta, out):
             )
 
         acc = {}
+        rs = {}
+        tr = {}
 
         def mx(g, m):
             if g == 0:
@@ -110,27 +109,32 @@ def tile_gdn_w_kernel(tc, x, gamma_words, gamma_scales, beta, out):
                 stop=(g == G - 1),
             )
 
-        def epilogue(m):
-            t = work.tile([P, 4, P], F32, name="t%d" % m, tag="t")
+        def rsqrt(m):
+            rs[m] = work.tile([P, 4, P], F32, name="rs%d" % m, tag="rs")
             nc.vector.tensor_tensor(
-                out=t[:], in0=acc[m][:].rearrange("n (v i) -> n i v", i=4), in1=beta_bc[:, m], op=ALU.add
+                out=rs[m][:], in0=acc[m][:].rearrange("n (v i) -> n i v", i=4), in1=beta_bc[:, m], op=ALU.add
             )
-            r = work.tile([P, 4, P], F32, name="r%d" % m, tag="r")
-            nc.scalar.activation(out=r[:], in_=t[:], func=ACT.Abs_reciprocal_sqrt)
-            tr = psum.tile([P, 4, P], F32, tag="bank%d" % m, name="tr%d" % m)
+            nc.scalar.activation(out=rs[m][:], in_=rs[m][:], func=ACT.Abs_reciprocal_sqrt)
+
+        def finish(m):
+            tr[m] = psum.tile([P, 4, P], F32, tag="bank%d" % m, name="tr%d" % m)
             for i in range(4):
-                nc.tensor.transpose(tr[:, i, :], r[:, i, :], ident[:])
+                nc.tensor.transpose(tr[m][:, i, :], rs[m][:, i, :], ident[:])
             o = outp.tile([P, 4, P], F32, name="o%d" % m, tag="o")
-            nc.vector.tensor_tensor(out=o[:], in0=tr[:], in1=xk4[:, m], op=ALU.mult)
+            nc.vector.tensor_tensor(out=o[:], in0=tr[m][:], in1=xk4[:, m], op=ALU.mult)
             nc.sync.dma_start(out=ov[:, m, :], in_=o[:].rearrange("p t n -> p (t n)"))
 
         for g in range(G):
             for m in range(4):
                 mx(g, m)
+        for m in range(4):
+            rsqrt(m)
         for g in range(G):
             for m in range(4, 8):
                 mx(g, m)
             if g < 4:
-                epilogue(g)
+                finish(g)
         for m in range(4, 8):
-            epilogue(m)
+            rsqrt(m)
+        for m in range(4, 8):
+            finish(m)

@@ -24,11 +24,13 @@ def tile_gdn_w_kernel(tc, x, gamma_words, gamma_scales, beta, out):
     nc = tc.nc
     xv = x.rearrange("b c h w -> (b c) (h w)").rearrange("(g p t) n -> p g (t n)", p=P, t=4)
     ov = out.rearrange("b c h w -> (b c) (h w)").rearrange("(g p t) n -> p g (t n)", p=P, t=4)
+    ov4 = out.rearrange("b c h w -> (b c) (h w)").rearrange("(g p t) n -> p g t n", p=P, t=4)
     with ExitStack() as ctx:
         ctx.enter_context(tc.manual_schedule())
         keep = ctx.enter_context(tc.tile_pool(name="keep", bufs=1))
         work = ctx.enter_context(tc.tile_pool(name="work", bufs=6))
-        outp = ctx.enter_context(tc.tile_pool(name="outp", bufs=8))
+        outp = ctx.enter_context(tc.tile_pool(name="outp", bufs=7))
+        last = ctx.enter_context(tc.tile_pool(name="last", bufs=4))
         psum = ctx.enter_context(tc.psum_pool(name="psum", bufs=1))
 
         planes = keep.tile([P, 2 * C], U8, align_bytes=64)
@@ -66,10 +68,10 @@ def tile_gdn_w_kernel(tc, x, gamma_words, gamma_scales, beta, out):
 
         for g in range(G):
             load_words(g, 0, 4)
-        for g in range(G - 1):
-            load_words(g, 4, 8)
-        for m in range(4, 8):
-            load_words(G - 1, m, m + 1)
+        for g in range(G):
+            load_words(g, 4, 7)
+        for g in range(G):
+            load_words(g, 7, 8)
 
         beta_bc = keep.tile([P, G, 4, P], F32)
         for m in range(G):
@@ -124,17 +126,43 @@ def tile_gdn_w_kernel(tc, x, gamma_words, gamma_scales, beta, out):
             nc.vector.tensor_tensor(out=o[:], in0=tr[m][:], in1=xk4[:, m], op=ALU.mult)
             nc.sync.dma_start(out=ov[:, m, :], in_=o[:].rearrange("p t n -> p (t n)"))
 
+        def rsqrt_slice(i):
+            rs[(7, i)] = last.tile([P, P], F32, name="rl%d" % i, tag="rl")
+            nc.vector.tensor_tensor(
+                out=rs[(7, i)][:],
+                in0=acc[7][:].rearrange("n (v i) -> n i v", i=4)[:, i, :],
+                in1=beta_bc[:, 7, i, :],
+                op=ALU.add,
+            )
+            nc.scalar.activation(out=rs[(7, i)][:], in_=rs[(7, i)][:], func=ACT.Abs_reciprocal_sqrt)
+
+        def finish_slice(i):
+            tl = psum.tile([P, P], F32, tag="bank%d" % i, name="tl%d" % i)
+            nc.tensor.transpose(tl[:], rs[(7, i)][:], ident[:])
+            o = last.tile([P, P], F32, name="ol%d" % i, tag="ol")
+            nc.vector.tensor_tensor(out=o[:], in0=tl[:], in1=xk4[:, 7, i, :], op=ALU.mult)
+            nc.sync.dma_start(out=ov4[:, 7, i, :], in_=o[:])
+
         for g in range(G):
             for m in range(4):
                 mx(g, m)
         for m in range(4):
             rsqrt(m)
         for g in range(G):
-            for m in range(4, 8):
+            for m in range(4, 7):
                 mx(g, m)
             if g < 4:
                 finish(g)
-        for m in range(4, 8):
+        for m in range(4, 7):
             rsqrt(m)
-        for m in range(4, 8):
+        for g in range(3):
+            mx(g, 7)
+        for m in range(4, 7):
             finish(m)
+            mx(m - 1, 7)
+        mx(6, 7)
+        mx(7, 7)
+        for i in range(4):
+            rsqrt_slice(i)
+        for i in range(4):
+            finish_slice(i)

@@ -18,13 +18,14 @@ P = 128
 C = 4096
 G = 8
 NB = 512
+LAST = 7
 
 
 def tile_gdn_w_kernel(tc, x, gamma_words, gamma_scales, beta, out):
     nc = tc.nc
     xv = x.rearrange("b c h w -> (b c) (h w)").rearrange("(g p t) n -> p g (t n)", p=P, t=4)
-    ov = out.rearrange("b c h w -> (b c) (h w)").rearrange("(g p t) n -> p g (t n)", p=P, t=4)
-    ov4 = out.rearrange("b c h w -> (b c) (h w)").rearrange("(g p t) n -> p g t n", p=P, t=4)
+    of = out.rearrange("b c h w -> (b c) (h w)")
+    ov = of.rearrange("(g p t) n -> p g (t n)", p=P, t=4)
     with ExitStack() as ctx:
         ctx.enter_context(tc.manual_schedule())
         keep = ctx.enter_context(tc.tile_pool(name="keep", bufs=1))
@@ -44,14 +45,16 @@ def tile_gdn_w_kernel(tc, x, gamma_words, gamma_scales, beta, out):
         warm = keep.tile([P, 1], F32)
         nc.scalar.activation(out=warm[:], in_=seed[:], func=ACT.Abs_reciprocal_sqrt)
         nc.scalar.dma_start(out=brow[0:1, :], in_=beta.rearrange("(o c) -> o c", o=1))
+        ident = keep.tile([P, P], F32)
+        make_identity(nc, ident[:])
+        identb = keep.tile([P, P], BF16)
+        make_identity(nc, identb[:])
         for a in range(2):
             for q in range(4):
                 nc.gpsimd.dma_start(
                     out=planes[32 * q : 32 * q + 16, a * C : (a + 1) * C].bitcast(F32),
                     in_=gamma_scales[4 * a : 4 * a + 4, 4 * q : 4 * q + 4, :].bitcast(F32),
                 )
-        ident = keep.tile([P, P], F32)
-        make_identity(nc, ident[:])
 
         xk = keep.tile([P, G, NB], BF16)
         nc.sync.dma_start(out=xk[:], in_=xv)
@@ -69,15 +72,21 @@ def tile_gdn_w_kernel(tc, x, gamma_words, gamma_scales, beta, out):
         for g in range(G):
             load_words(g, 0, 4)
         for g in range(G):
-            load_words(g, 4, 7)
+            load_words(g, 4, LAST)
         for g in range(G):
-            load_words(g, 7, 8)
+            load_words(g, LAST, LAST + 1)
 
-        beta_bc = keep.tile([P, G, 4, P], F32)
-        for m in range(G):
+        beta_bc = keep.tile([P, LAST, 4, P], F32)
+        for m in range(LAST):
             bp = psum.tile([P, NB], F32, tag="bank%d" % m, name="bp%d" % m)
             nc.tensor.matmul(out=bp[:], lhsT=ones[:], rhs=brow[:, m * NB : (m + 1) * NB], start=True, stop=True)
             nc.scalar.copy(out=beta_bc[:, m], in_=bp[:].rearrange("n (v i) -> n i v", i=4))
+        pb = psum.tile([P, 4, 32], F32, tag="bank7", name="pb")
+        for s in range(4):
+            c0 = LAST * NB + s * P
+            nc.tensor.matmul(out=pb[:, s, :], lhsT=brow[:, c0 : c0 + P], rhs=ones[:, 0:32], start=True, stop=True)
+        beta_col = keep.tile([P, 4], F32)
+        nc.scalar.copy(out=beta_col[:], in_=pb[:, :, 0])
 
         xk4 = xk[:].rearrange("p g (t n) -> p g t n", t=4)
         grouped = keep.tile([P, G, P, 4], BF16, align_bytes=64)
@@ -126,43 +135,70 @@ def tile_gdn_w_kernel(tc, x, gamma_words, gamma_scales, beta, out):
             nc.vector.tensor_tensor(out=o[:], in0=tr[m][:], in1=xk4[:, m], op=ALU.mult)
             nc.sync.dma_start(out=ov[:, m, :], in_=o[:].rearrange("p t n -> p (t n)"))
 
-        def rsqrt_slice(i):
-            rs[(7, i)] = last.tile([P, P], F32, name="rl%d" % i, tag="rl")
-            nc.vector.tensor_tensor(
-                out=rs[(7, i)][:],
-                in0=acc[7][:].rearrange("n (v i) -> n i v", i=4)[:, i, :],
-                in1=beta_bc[:, 7, i, :],
-                op=ALU.add,
-            )
-            nc.scalar.activation(out=rs[(7, i)][:], in_=rs[(7, i)][:], func=ACT.Abs_reciprocal_sqrt)
+        def mx_last(g):
+            a, b = divmod(g, 4)
+            for s in range(4):
+                if g == 0:
+                    acc[(LAST, s)] = psum.tile([P, P], F32, tag="bank%d" % s, name="accl%d" % s)
+                c0 = a * C + LAST * NB + s * P
+                nc.tensor.matmul_mx(
+                    out=acc[(LAST, s)][:],
+                    lhsT=words[(g, LAST)][:, s * P : (s + 1) * P].bitcast(FP8X4),
+                    lhsT_scale=planes[4 * b : P, c0 : c0 + P],
+                    rhs=codes[:, g * P : (g + 1) * P].bitcast(FP8X4),
+                    rhs_scale=sqplane[:, g * P : (g + 1) * P],
+                    start=(g == 0),
+                    stop=(g == G - 1),
+                )
 
-        def finish_slice(i):
-            tl = psum.tile([P, P], F32, tag="bank%d" % i, name="tl%d" % i)
-            nc.tensor.transpose(tl[:], rs[(7, i)][:], ident[:])
-            o = last.tile([P, P], F32, name="ol%d" % i, tag="ol")
-            nc.vector.tensor_tensor(out=o[:], in0=tl[:], in1=xk4[:, 7, i, :], op=ALU.mult)
-            nc.sync.dma_start(out=ov4[:, 7, i, :], in_=o[:])
+        xt = keep.tile([P, P, 4], BF16)
+        xcol = keep.tile([P, 4, P], BF16)
+
+        def x_last_first_half():
+            pt = psum.tile([P, 4, P], BF16, tag="bank7", name="pt")
+            for t in range(4):
+                nc.tensor.transpose(pt[:, t, :], xk4[:, LAST, t, :], identb[:])
+            nc.scalar.copy(out=xt[:], in_=pt[:].rearrange("n t p -> n p t"))
+
+        def x_last_second_half():
+            po = psum.tile([P, 4, P], BF16, tag="bank7", name="po")
+            flat = xt[:].rearrange("n p t -> n (p t)")
+            for s in range(4):
+                nc.tensor.transpose(po[:, s, :], flat[:, s * P : (s + 1) * P], identb[:])
+            nc.scalar.copy(out=xcol[:], in_=po[:])
+
+        def finish_last(s):
+            r = last.tile([P, P], F32, name="rl%d" % s, tag="rl")
+            nc.scalar.activation(
+                out=r[:], in_=acc[(LAST, s)][:], func=ACT.Abs_reciprocal_sqrt, bias=beta_col[:, s : s + 1]
+            )
+            o = last.tile([P, P], F32, name="ol%d" % s, tag="ol")
+            nc.vector.tensor_tensor(out=o[:], in0=r[:], in1=xcol[:, s, :], op=ALU.mult)
+            c0 = LAST * NB + s * P
+            nc.sync.dma_start(out=of[c0 : c0 + P, :], in_=o[:])
 
         for g in range(G):
             for m in range(4):
                 mx(g, m)
+            if g == 1:
+                x_last_first_half()
+            if g == 3:
+                x_last_second_half()
         for m in range(4):
             rsqrt(m)
         for g in range(G):
-            for m in range(4, 7):
+            for m in range(4, LAST):
                 mx(g, m)
             if g < 4:
                 finish(g)
-        for m in range(4, 7):
+        for m in range(4, LAST):
             rsqrt(m)
         for g in range(3):
-            mx(g, 7)
-        for m in range(4, 7):
+            mx_last(g)
+        for m in range(4, LAST):
             finish(m)
-            mx(m - 1, 7)
-        mx(6, 7)
-        mx(7, 7)
-        for i in range(4):
-            rsqrt_slice(i)
-        for i in range(4):
-            finish_slice(i)
+            mx_last(m - 1)
+        mx_last(6)
+        mx_last(7)
+        for s in range(4):
+            finish_last(s)

@@ -73,8 +73,17 @@ def tile_gdn_w_kernel(tc, x, gamma_words, gamma_scales, beta, out):
             load_words(g, 0, 4)
         for g in range(G):
             load_words(g, 4, LAST)
-        for g in range(G):
+        for g in range(G - 1):
             load_words(g, LAST, LAST + 1)
+        halves = []
+        for h in range(2):
+            t = keep.tile([P, NB // 2], U32, name="wlast%d" % h, align_bytes=64)
+            c0 = LAST * NB + h * (NB // 2)
+            nc.sync.dma_start(
+                out=t[:].bitcast(I32),
+                in_=gamma_words[G - 1, :, c0 : c0 + NB // 2, :].rearrange("p n t -> p (n t)").bitcast(I32),
+            )
+            halves.append(t)
 
         beta_bc = keep.tile([P, LAST, 4, P], F32)
         for m in range(LAST):
@@ -143,7 +152,11 @@ def tile_gdn_w_kernel(tc, x, gamma_words, gamma_scales, beta, out):
                 c0 = a * C + LAST * NB + s * P
                 nc.tensor.matmul_mx(
                     out=acc[(LAST, s)][:],
-                    lhsT=words[(g, LAST)][:, s * P : (s + 1) * P].bitcast(FP8X4),
+                    lhsT=(
+                        words[(g, LAST)][:, s * P : (s + 1) * P]
+                        if g < G - 1
+                        else halves[s // 2][:, (s % 2) * P : (s % 2 + 1) * P]
+                    ).bitcast(FP8X4),
                     lhsT_scale=planes[4 * b : P, c0 : c0 + P],
                     rhs=codes[:, g * P : (g + 1) * P].bitcast(FP8X4),
                     rhs_scale=sqplane[:, g * P : (g + 1) * P],

from contextlib import ExitStack

import concourse.mybir as mybir
from concourse.masks import make_identity

FLOPS = 2 * 4096 * 4096 * 128

F32 = mybir.dt.float32
BF16 = mybir.dt.bfloat16
I32 = mybir.dt.int32
U32 = mybir.dt.uint32
U8 = mybir.dt.uint8
FP8X4 = mybir.dt.float8_e4m3fn_x4
ACT = mybir.ActivationFunctionType
ALU = mybir.AluOpType

P = 128
C = 4096
G = 8
NB = 512
LAST = 7


def tile_gdn_w_kernel(tc, x, gamma_words, gamma_scales, beta, out):
    nc = tc.nc
    xv = x.rearrange("b c h w -> (b c) (h w)").rearrange("(g p t) n -> p g (t n)", p=P, t=4)
    of = out.rearrange("b c h w -> (b c) (h w)")
    ov = of.rearrange("(g p t) n -> p g (t n)", p=P, t=4)
    with ExitStack() as ctx:
        ctx.enter_context(tc.manual_schedule())
        keep = ctx.enter_context(tc.tile_pool(name="keep", bufs=1))
        work = ctx.enter_context(tc.tile_pool(name="work", bufs=6))
        outp = ctx.enter_context(tc.tile_pool(name="outp", bufs=7))
        last = ctx.enter_context(tc.tile_pool(name="last", bufs=4))
        psum = ctx.enter_context(tc.psum_pool(name="psum", bufs=1))

        planes = keep.tile([P, 2 * C], U8, align_bytes=64)
        nc.vector.memset(planes[:].bitcast(I32), 0)
        brow = keep.tile([P, C], BF16)
        nc.vector.memset(brow[:].bitcast(I32), 0)
        ones = keep.tile([P, P], BF16)
        nc.vector.memset(ones[:], 1.0)
        seed = keep.tile([P, 1], F32)
        nc.vector.memset(seed[:], 1.0)
        warm = keep.tile([P, 1], F32)
        nc.scalar.activation(out=warm[:], in_=seed[:], func=ACT.Abs_reciprocal_sqrt)
        nc.scalar.dma_start(out=brow[0:1, :], in_=beta.rearrange("(o c) -> o c", o=1))
        ident = keep.tile([P, P], F32)
        make_identity(nc, ident[:])
        identb = keep.tile([P, P], BF16)
        make_identity(nc, identb[:])
        for a in range(2):
            for q in range(4):
                nc.gpsimd.dma_start(
                    out=planes[32 * q : 32 * q + 16, a * C : (a + 1) * C].bitcast(F32),
                    in_=gamma_scales[4 * a : 4 * a + 4, 4 * q : 4 * q + 4, :].bitcast(F32),
                )

        xk = keep.tile([P, G, NB], BF16)
        nc.sync.dma_start(out=xk[:], in_=xv)
        words = {}

        def load_words(g, m0, m1):
            t = keep.tile([P, (m1 - m0) * NB], U32, name="w%d_%d" % (g, m0), align_bytes=64)
            nc.sync.dma_start(
                out=t[:].bitcast(I32),
                in_=gamma_words[g, :, m0 * NB : m1 * NB, :].rearrange("p n t -> p (n t)").bitcast(I32),
            )
            for m in range(m0, m1):
                words[(g, m)] = t[:, (m - m0) * NB : (m - m0 + 1) * NB]

        for g in range(G):
            load_words(g, 0, 4)
        for g in range(G):
            load_words(g, 4, LAST)
        for g in range(G - 1):
            load_words(g, LAST, LAST + 1)
        halves = []
        for h in range(2):
            t = keep.tile([P, NB // 2], U32, name="wlast%d" % h, align_bytes=64)
            c0 = LAST * NB + h * (NB // 2)
            nc.sync.dma_start(
                out=t[:].bitcast(I32),
                in_=gamma_words[G - 1, :, c0 : c0 + NB // 2, :].rearrange("p n t -> p (n t)").bitcast(I32),
            )
            halves.append(t)

        beta_bc = keep.tile([P, LAST, 4, P], F32)
        for m in range(LAST):
            bp = psum.tile([P, NB], F32, tag="bank%d" % m, name="bp%d" % m)
            nc.tensor.matmul(out=bp[:], lhsT=ones[:], rhs=brow[:, m * NB : (m + 1) * NB], start=True, stop=True)
            nc.scalar.copy(out=beta_bc[:, m], in_=bp[:].rearrange("n (v i) -> n i v", i=4))
        pb = psum.tile([P, 4, 32], F32, tag="bank7", name="pb")
        for s in range(4):
            c0 = LAST * NB + s * P
            nc.tensor.matmul(out=pb[:, s, :], lhsT=brow[:, c0 : c0 + P], rhs=ones[:, 0:32], start=True, stop=True)
        beta_col = keep.tile([P, 4], F32)
        nc.scalar.copy(out=beta_col[:], in_=pb[:, :, 0])

        xk4 = xk[:].rearrange("p g (t n) -> p g t n", t=4)
        grouped = keep.tile([P, G, P, 4], BF16, align_bytes=64)
        codes = keep.tile([P, G * P], U32, align_bytes=64)
        sqplane = keep.tile([P, G * P], U8, align_bytes=64)
        for h in range(2):
            src = xk4[:, 4 * h : 4 * h + 4].rearrange("p g t n -> p g n t")
            nc.vector.tensor_tensor(out=grouped[:, 4 * h : 4 * h + 4], in0=src, in1=src, op=ALU.mult)
        for h in range(2):
            nc.vector.quantize_mx(
                out=codes[:, 512 * h : 512 * (h + 1)].bitcast(FP8X4),
                scales=sqplane[:, 512 * h : 512 * (h + 1)],
                in_=grouped[:, 4 * h : 4 * h + 4].rearrange("p g n t -> p (g n t)"),
            )

        acc = {}
        rs = {}
        tr = {}

        def mx(g, m):
            if g == 0:
                acc[m] = psum.tile([P, NB], F32, tag="bank%d" % m, name="acc%d" % m)
            a, b = divmod(g, 4)
            nc.tensor.matmul_mx(
                out=acc[m][:],
                lhsT=codes[:, g * P : (g + 1) * P].bitcast(FP8X4),
                lhsT_scale=sqplane[:, g * P : (g + 1) * P],
                rhs=words[(g, m)].bitcast(FP8X4),
                rhs_scale=planes[4 * b : P, a * C + m * NB : a * C + (m + 1) * NB],
                start=(g == 0),
                stop=(g == G - 1),
            )

        def rsqrt(m):
            rs[m] = work.tile([P, 4, P], F32, name="rs%d" % m, tag="rs")
            nc.vector.tensor_tensor(
                out=rs[m][:], in0=acc[m][:].rearrange("n (v i) -> n i v", i=4), in1=beta_bc[:, m], op=ALU.add
            )
            nc.scalar.activation(out=rs[m][:], in_=rs[m][:], func=ACT.Abs_reciprocal_sqrt)

        def finish(m):
            tr[m] = psum.tile([P, 4, P], F32, tag="bank%d" % m, name="tr%d" % m)
            for i in range(4):
                nc.tensor.transpose(tr[m][:, i, :], rs[m][:, i, :], ident[:])
            o = outp.tile([P, 4, P], F32, name="o%d" % m, tag="o")
            nc.vector.tensor_tensor(out=o[:], in0=tr[m][:], in1=xk4[:, m], op=ALU.mult)
            nc.sync.dma_start(out=ov[:, m, :], in_=o[:].rearrange("p t n -> p (t n)"))

        def mx_last(g):
            a, b = divmod(g, 4)
            for s in range(4):
                if g == 0:
                    acc[(LAST, s)] = psum.tile([P, P], F32, tag="bank%d" % s, name="accl%d" % s)
                c0 = a * C + LAST * NB + s * P
                nc.tensor.matmul_mx(
                    out=acc[(LAST, s)][:],
                    lhsT=(
                        words[(g, LAST)][:, s * P : (s + 1) * P]
                        if g < G - 1
                        else halves[s // 2][:, (s % 2) * P : (s % 2 + 1) * P]
                    ).bitcast(FP8X4),
                    lhsT_scale=planes[4 * b : P, c0 : c0 + P],
                    rhs=codes[:, g * P : (g + 1) * P].bitcast(FP8X4),
                    rhs_scale=sqplane[:, g * P : (g + 1) * P],
                    start=(g == 0),
                    stop=(g == G - 1),
                )

        xt = keep.tile([P, P, 4], BF16)
        xcol = keep.tile([P, 4, P], BF16)

        def x_last_first_half():
            pt = psum.tile([P, 4, P], BF16, tag="bank7", name="pt")
            for t in range(4):
                nc.tensor.transpose(pt[:, t, :], xk4[:, LAST, t, :], identb[:])
            nc.scalar.copy(out=xt[:], in_=pt[:].rearrange("n t p -> n p t"))

        def x_last_second_half():
            po = psum.tile([P, 4, P], BF16, tag="bank7", name="po")
            flat = xt[:].rearrange("n p t -> n (p t)")
            for s in range(4):
                nc.tensor.transpose(po[:, s, :], flat[:, s * P : (s + 1) * P], identb[:])
            nc.scalar.copy(out=xcol[:], in_=po[:])

        def finish_last(s):
            r = last.tile([P, P], F32, name="rl%d" % s, tag="rl")
            nc.scalar.activation(
                out=r[:], in_=acc[(LAST, s)][:], func=ACT.Abs_reciprocal_sqrt, bias=beta_col[:, s : s + 1]
            )
            o = last.tile([P, P], F32, name="ol%d" % s, tag="ol")
            nc.vector.tensor_tensor(out=o[:], in0=r[:], in1=xcol[:, s, :], op=ALU.mult)
            c0 = LAST * NB + s * P
            nc.sync.dma_start(out=of[c0 : c0 + P, :], in_=o[:])

        for g in range(G):
            for m in range(4):
                mx(g, m)
            if g == 1:
                x_last_first_half()
            if g == 3:
                x_last_second_half()
        for m in range(4):
            rsqrt(m)
        for g in range(G):
            for m in range(4, LAST):
                mx(g, m)
            if g < 4:
                finish(g)
        for m in range(4, LAST):
            rsqrt(m)
        for g in range(3):
            mx_last(g)
        for m in range(4, LAST):
            finish(m)
            mx_last(m - 1)
        mx_last(6)
        mx_last(7)
        for s in range(4):
            finish_last(s)
